import numpy as np
import ml_dtypes

BF16 = ml_dtypes.bfloat16


def bf(x):
    return np.asarray(x, np.float32).astype(BF16)


def f32(x):
    return np.asarray(x, np.float32)


def f64(x):
    return np.asarray(x).astype(np.float64)


def striped(idx):
    return np.tile(idx.reshape(-1, 16).T, (8, 1))


D, S, M, H1, H2, N = 128, 256, 256, 512, 256, 512
SLOPE = 0.01


def lrelu(t):
    return np.maximum(t, SLOPE * t)


def setup_inputs():
    return {
        "table": bf(np.random.standard_normal((D, S))),
        "w": bf(np.random.standard_normal((D, M)) / np.sqrt(D)),
        "bv": f32(0.1 * np.random.standard_normal((M, 1))),
        "w1": bf(np.random.standard_normal((M, H1)) / np.sqrt(M)),
        "b1": f32(0.1 * np.random.standard_normal((H1, 1))),
        "w2": bf(np.random.standard_normal((H1, H2)) / np.sqrt(H1)),
        "b2": f32(0.1 * np.random.standard_normal((H2, 1))),
        "offs": striped(np.random.permutation(np.tile(np.arange(S), 2))[:N]),
    }


def reference(table, w, bv, w1, b1, w2, b2, offs):
    idx = offs[:16].T.reshape(-1)
    v = f64(w).T @ f64(table)[:, idx] + f64(bv)
    h = lrelu(f64(w1).T @ v + f64(b1))
    return lrelu(f64(w2).T @ h + f64(b2))

@@ -1,0 +1,86 @@
+import concourse.mybir as mybir
+
+BF16, F32, U16 = mybir.dt.bfloat16, mybir.dt.float32, mybir.dt.uint16
+IDENTITY = mybir.ActivationFunctionType.Identity
+ADD, MULT, MAX = mybir.AluOpType.add, mybir.AluOpType.mult, mybir.AluOpType.max
+
+P = 128
+D, S, M, H1, H2, N = 128, 256, 256, 512, 256, 512
+SLOPE = 0.01
+PIECE = 256
+FLOPS = 2 * N * (D * M + M * H1 + H1 * H2)
+
+
+def bias_lrelu(nc, work, dest, product, bias_column):
+    shifted = work.tile([P, N], F32, name="shifted")
+    nc.scalar.activation(shifted[:], product, IDENTITY, bias=bias_column)
+    nc.vector.scalar_tensor_tensor(dest, shifted[:], SLOPE, shifted[:], MULT, MAX)
+
+
+def tile_textclassifier_kernel(tc, table, w, bv, w1, b1, w2, b2, offs, out):
+    nc = tc.nc
+    with (
+        tc.tile_pool(name="held", bufs=1) as held,
+        tc.tile_pool(name="work", bufs=3) as work,
+        tc.psum_pool(name="psum_v", bufs=2) as psum_v,
+        tc.psum_pool(name="psum_h", bufs=4) as psum_h,
+        tc.psum_pool(name="psum_o", bufs=2) as psum_o,
+    ):
+        offsets = held.tile([P, N // 16], U16, name="offsets")
+        nc.sync.dma_start(offsets[:], offs)
+        table_sb = held.tile([P, S], BF16, name="table_sb")
+        nc.sync.dma_start(table_sb[:], table)
+        w_sb = held.tile([P, M], BF16, name="w_sb")
+        nc.scalar.dma_start(w_sb[:], w)
+        w1_sb = held.tile([P, M // P, H1], BF16, name="w1_sb")
+        nc.sync.dma_start(w1_sb[:], w1.rearrange("(k p) n -> p k n", p=P))
+        w2_sb = held.tile([P, H1 // P, H2], BF16, name="w2_sb")
+        nc.scalar.dma_start(w2_sb[:], w2.rearrange("(k p) n -> p k n", p=P))
+        bv_sb = held.tile([P, M // P], F32, name="bv_sb")
+        b1_sb = held.tile([P, H1 // P], F32, name="b1_sb")
+        b2_sb = held.tile([P, H2 // P], F32, name="b2_sb")
+        with nc.allow_non_contiguous_dma(reason="a bias has one element to a partition"):
+            nc.gpsimd.dma_start(bv_sb[:], bv.rearrange("(k p) o -> p (k o)", p=P))
+            nc.gpsimd.dma_start(b1_sb[:], b1.rearrange("(k p) o -> p (k o)", p=P))
+            nc.gpsimd.dma_start(b2_sb[:], b2.rearrange("(k p) o -> p (k o)", p=P))
+
+        v_bf = held.tile([P, M // P, N], BF16, name="v_bf")
+        for m in range(M // P):
+            v_ps = psum_v.tile([P, N], F32, name="v_ps")
+            for c in range(N // PIECE):
+                picked = table_sb[:].indirect(offsets[:, c * (PIECE // 16) : (c + 1) * (PIECE // 16)])
+                nc.tensor.matmul(
+                    v_ps[:, c * PIECE : (c + 1) * PIECE],
+                    w_sb[:, m * P : (m + 1) * P],
+                    picked,
+                    start=True,
+                    stop=True,
+                )
+            nc.vector.tensor_scalar(v_bf[:, m, :], v_ps[:], bv_sb[:, m : m + 1], None, ADD)
+
+        h_bf = held.tile([P, H1 // P, N], BF16, name="h_bf")
+        for p in range(H1 // P):
+            h_ps = psum_h.tile([P, N], F32, name="h_ps")
+            for k in range(M // P):
+                nc.tensor.matmul(
+                    h_ps[:],
+                    w1_sb[:, k, p * P : (p + 1) * P],
+                    v_bf[:, k, :],
+                    start=(k == 0),
+                    stop=(k == M // P - 1),
+                )
+            bias_lrelu(nc, work, h_bf[:, p, :], h_ps[:], b1_sb[:, p : p + 1])
+
+        for r in range(H2 // P):
+            o_ps = psum_o.tile([P, N], F32, name="o_ps")
+            for k in range(H1 // P):
+                nc.tensor.matmul(
+                    o_ps[:],
+                    w2_sb[:, k, r * P : (r + 1) * P],
+                    h_bf[:, k, :],
+                    start=(k == 0),
+                    stop=(k == H1 // P - 1),
+                )
+            o_sb = work.tile([P, N], F32, name="o_sb")
+            bias_lrelu(nc, work, o_sb[:], o_ps[:], b2_sb[:, r : r + 1])
+            nc.sync.dma_start(out[r * P : (r + 1) * P, :], o_sb[:])

@@ -8,11 +8,12 @@ P = 128
 D, S, M, H1, H2, N = 128, 256, 256, 512, 256, 512
 SLOPE = 0.01
 PIECE = 256
+PIECES = N // PIECE
 FLOPS = 2 * N * (D * M + M * H1 + H1 * H2)
 
 
 def bias_lrelu(nc, work, dest, product, bias_column):
-    shifted = work.tile([P, N], F32, name="shifted")
+    shifted = work.tile([P, PIECE], F32, name="shifted")
     nc.scalar.activation(shifted[:], product, IDENTITY, bias=bias_column)
     nc.vector.scalar_tensor_tensor(dest, shifted[:], SLOPE, shifted[:], MULT, MAX)
 
@@ -21,10 +22,8 @@ def tile_textclassifier_kernel(tc, table, w, bv, w1, b1, w2, b2, offs, out):
     nc = tc.nc
     with (
         tc.tile_pool(name="held", bufs=1) as held,
-        tc.tile_pool(name="work", bufs=3) as work,
-        tc.psum_pool(name="psum_v", bufs=2) as psum_v,
-        tc.psum_pool(name="psum_h", bufs=4) as psum_h,
-        tc.psum_pool(name="psum_o", bufs=2) as psum_o,
+        tc.tile_pool(name="work", bufs=4) as work,
+        tc.psum_pool(name="psum", bufs=8) as psum,
     ):
         offsets = held.tile([P, N // 16], U16, name="offsets")
         nc.sync.dma_start(offsets[:], offs)
@@ -32,55 +31,65 @@ def tile_textclassifier_kernel(tc, table, w, bv, w1, b1, w2, b2, offs, out):
         nc.sync.dma_start(table_sb[:], table)
         w_sb = held.tile([P, M], BF16, name="w_sb")
         nc.scalar.dma_start(w_sb[:], w)
-        w1_sb = held.tile([P, M // P, H1], BF16, name="w1_sb")
-        nc.sync.dma_start(w1_sb[:], w1.rearrange("(k p) n -> p k n", p=P))
-        w2_sb = held.tile([P, H1 // P, H2], BF16, name="w2_sb")
-        nc.scalar.dma_start(w2_sb[:], w2.rearrange("(k p) n -> p k n", p=P))
-        bv_sb = held.tile([P, M // P], F32, name="bv_sb")
-        b1_sb = held.tile([P, H1 // P], F32, name="b1_sb")
-        b2_sb = held.tile([P, H2 // P], F32, name="b2_sb")
-        with nc.allow_non_contiguous_dma(reason="a bias has one element to a partition"):
-            nc.gpsimd.dma_start(bv_sb[:], bv.rearrange("(k p) o -> p (k o)", p=P))
-            nc.gpsimd.dma_start(b1_sb[:], b1.rearrange("(k p) o -> p (k o)", p=P))
-            nc.gpsimd.dma_start(b2_sb[:], b2.rearrange("(k p) o -> p (k o)", p=P))
 
-        v_bf = held.tile([P, M // P, N], BF16, name="v_bf")
-        for m in range(M // P):
-            v_ps = psum_v.tile([P, N], F32, name="v_ps")
-            for c in range(N // PIECE):
-                picked = table_sb[:].indirect(offsets[:, c * (PIECE // 16) : (c + 1) * (PIECE // 16)])
+        bv_sb = held.tile([P, M // P], F32, name="bv_sb")
+        with nc.allow_non_contiguous_dma(reason="bv has one element to a partition and block"):
+            nc.scalar.dma_start(bv_sb[:], bv.rearrange("(k p) o -> p (k o)", p=P))
+        w1_sb = held.tile([P, M // P, H1], BF16, name="w1_sb")
+
+        b1_sb = held.tile([P, H1 // P], F32, name="b1_sb")
+        nc.sync.dma_start(b1_sb[:], b1.rearrange("(p b) o -> p (b o)", p=P))
+        nc.sync.dma_start(w1_sb[:], w1.rearrange("(k p) n -> p k n", p=P))
+        b2_sb = held.tile([P, H2 // P], F32, name="b2_sb")
+        nc.scalar.dma_start(b2_sb[:], b2.rearrange("(p b) o -> p (b o)", p=P))
+        w2_sb = held.tile([P, H1 // P, H2], BF16, name="w2_sb")
+        nc.scalar.dma_start(w2_sb[:], w2.rearrange("(p k) n -> p k n", p=P))
+        w1_blocks = w1_sb[:].rearrange("d k (p b) -> d k b p", p=P)
+        w2_blocks = w2_sb[:].rearrange("d k (p b) -> d k b p", p=P)
+        out_blocks = out.rearrange("(p b) n -> p b n", p=P)
+
+        v_bf = [held.tile([P, M // P, PIECE], BF16, name=f"v_bf{c}") for c in range(PIECES)]
+        h_bf = [held.tile([P, H1 // P, PIECE], BF16, name=f"h_bf{c}") for c in range(PIECES)]
+
+        for c in range(PIECES):
+            for m in range(M // P):
+                v_ps = psum.tile([P, PIECE], F32, name="product")
                 nc.tensor.matmul(
-                    v_ps[:, c * PIECE : (c + 1) * PIECE],
+                    v_ps[:],
                     w_sb[:, m * P : (m + 1) * P],
-                    picked,
+                    table_sb[:].indirect(offsets[:, c * (PIECE // 16) : (c + 1) * (PIECE // 16)]),
                     start=True,
                     stop=True,
                 )
-            nc.vector.tensor_scalar(v_bf[:, m, :], v_ps[:], bv_sb[:, m : m + 1], None, ADD)
+                if m % 2 == 0:
+                    nc.scalar.activation(v_bf[c][:, m, :], v_ps[:], IDENTITY, bias=bv_sb[:, m : m + 1])
+                else:
+                    nc.vector.tensor_scalar(v_bf[c][:, m, :], v_ps[:], bv_sb[:, m : m + 1], None, ADD)
 
-        h_bf = held.tile([P, H1 // P, N], BF16, name="h_bf")
-        for p in range(H1 // P):
-            h_ps = psum_h.tile([P, N], F32, name="h_ps")
-            for k in range(M // P):
-                nc.tensor.matmul(
-                    h_ps[:],
-                    w1_sb[:, k, p * P : (p + 1) * P],
-                    v_bf[:, k, :],
-                    start=(k == 0),
-                    stop=(k == M // P - 1),
-                )
-            bias_lrelu(nc, work, h_bf[:, p, :], h_ps[:], b1_sb[:, p : p + 1])
+        for c in range(PIECES):
+            for b in range(H1 // P):
+                h_ps = psum.tile([P, PIECE], F32, name="product")
+                for k in range(M // P):
+                    nc.tensor.matmul(
+                        h_ps[:],
+                        w1_blocks[:, k, b, :],
+                        v_bf[c][:, k, :],
+                        start=(k == 0),
+                        stop=(k == M // P - 1),
+                    )
+                bias_lrelu(nc, work, h_bf[c][:, b, :], h_ps[:], b1_sb[:, b : b + 1])
 
-        for r in range(H2 // P):
-            o_ps = psum_o.tile([P, N], F32, name="o_ps")
-            for k in range(H1 // P):
-                nc.tensor.matmul(
-                    o_ps[:],
-                    w2_sb[:, k, r * P : (r + 1) * P],
-                    h_bf[:, k, :],
-                    start=(k == 0),
-                    stop=(k == H1 // P - 1),
-                )
-            o_sb = work.tile([P, N], F32, name="o_sb")
-            bias_lrelu(nc, work, o_sb[:], o_ps[:], b2_sb[:, r : r + 1])
-            nc.sync.dma_start(out[r * P : (r + 1) * P, :], o_sb[:])
+        for c in range(PIECES):
+            for b in range(H2 // P):
+                o_ps = psum.tile([P, PIECE], F32, name="product")
+                for k in range(H1 // P):
+                    nc.tensor.matmul(
+                        o_ps[:],
+                        w2_blocks[:, k, b, :],
+                        h_bf[c][:, k, :],
+                        start=(k == 0),
+                        stop=(k == H1 // P - 1),
+                    )
+                o_sb = work.tile([P, PIECE], F32, name="o_sb")
+                bias_lrelu(nc, work, o_sb[:], o_ps[:], b2_sb[:, b : b + 1])
+                nc.sync.dma_start(out_blocks[:, b, c * PIECE : (c + 1) * PIECE], o_sb[:])

@@ -9,6 +9,7 @@ D, S, M, H1, H2, N = 128, 256, 256, 512, 256, 512
 SLOPE = 0.01
 PIECE = 256
 PIECES = N // PIECE
+WARM_UP = 4
 FLOPS = 2 * N * (D * M + M * H1 + H1 * H2)
 
 
@@ -47,6 +48,12 @@ def tile_textclassifier_kernel(tc, table, w, bv, w1, b1, w2, b2, offs, out):
         w1_blocks = w1_sb[:].rearrange("d k (p b) -> d k b p", p=P)
         w2_blocks = w2_sb[:].rearrange("d k (p b) -> d k b p", p=P)
         out_blocks = out.rearrange("(p b) n -> p b n", p=P)
+
+        zeros = held.tile([P, N], BF16, name="zeros")
+        nc.vector.memset(zeros[:], 0.0)
+        warm_ps = psum.tile([P, N], F32, name="product")
+        for i in range(WARM_UP):
+            nc.tensor.matmul(warm_ps[:], zeros[:, 0:P], zeros[:], start=True, stop=True)
 
         v_bf = [held.tile([P, M // P, PIECE], BF16, name=f"v_bf{c}") for c in range(PIECES)]
         h_bf = [held.tile([P, H1 // P, PIECE], BF16, name=f"h_bf{c}") for c in range(PIECES)]

@@ -9,7 +9,7 @@ D, S, M, H1, H2, N = 128, 256, 256, 512, 256, 512
 SLOPE = 0.01
 PIECE = 256
 PIECES = N // PIECE
-WARM_UP = 4
+WARM_UP = 14
 FLOPS = 2 * N * (D * M + M * H1 + H1 * H2)
 
 
@@ -49,11 +49,14 @@ def tile_textclassifier_kernel(tc, table, w, bv, w1, b1, w2, b2, offs, out):
         w2_blocks = w2_sb[:].rearrange("d k (p b) -> d k b p", p=P)
         out_blocks = out.rearrange("(p b) n -> p b n", p=P)
 
-        zeros = held.tile([P, N], BF16, name="zeros")
+        zeros = held.tile([P, P], BF16, name="zeros")
         nc.vector.memset(zeros[:], 0.0)
-        warm_ps = psum.tile([P, N], F32, name="product")
+        warm_ps = psum.tile([P, P], F32, name="product")
         for i in range(WARM_UP):
-            nc.tensor.matmul(warm_ps[:], zeros[:, 0:P], zeros[:], start=True, stop=True)
+            nc.tensor.matmul(warm_ps[:], zeros[:], zeros[:], start=True, stop=True)
+
+        first_act = held.tile([P, 1], F32, name="first_act")
+        nc.scalar.activation(first_act[:], zeros[:, 0:1], IDENTITY)
 
         v_bf = [held.tile([P, M // P, PIECE], BF16, name=f"v_bf{c}") for c in range(PIECES)]
         h_bf = [held.tile([P, H1 // P, PIECE], BF16, name=f"h_bf{c}") for c in range(PIECES)]

@@ -14,9 +14,10 @@ FLOPS = 2 * N * (D * M + M * H1 + H1 * H2)
 
 
 def bias_lrelu(nc, work, dest, product, bias_column):
+    width = product.shape[1]
     shifted = work.tile([P, PIECE], F32, name="shifted")
-    nc.scalar.activation(shifted[:], product, IDENTITY, bias=bias_column)
-    nc.vector.scalar_tensor_tensor(dest, shifted[:], SLOPE, shifted[:], MULT, MAX)
+    nc.scalar.activation(shifted[:, :width], product, IDENTITY, bias=bias_column)
+    nc.vector.scalar_tensor_tensor(dest, shifted[:, :width], SLOPE, shifted[:, :width], MULT, MAX)
 
 
 def tile_textclassifier_kernel(tc, table, w, bv, w1, b1, w2, b2, offs, out):
@@ -90,16 +91,20 @@ def tile_textclassifier_kernel(tc, table, w, bv, w1, b1, w2, b2, offs, out):
                 bias_lrelu(nc, work, h_bf[c][:, b, :], h_ps[:], b1_sb[:, b : b + 1])
 
         for c in range(PIECES):
-            for b in range(H2 // P):
-                o_ps = psum.tile([P, PIECE], F32, name="product")
-                for k in range(H1 // P):
-                    nc.tensor.matmul(
-                        o_ps[:],
-                        w2_blocks[:, k, b, :],
-                        h_bf[c][:, k, :],
-                        start=(k == 0),
-                        stop=(k == H1 // P - 1),
-                    )
-                o_sb = work.tile([P, PIECE], F32, name="o_sb")
-                bias_lrelu(nc, work, o_sb[:], o_ps[:], b2_sb[:, b : b + 1])
-                nc.sync.dma_start(out_blocks[:, b, c * PIECE : (c + 1) * PIECE], o_sb[:])
+            cuts = 2 if c == PIECES - 1 else 1
+            width = PIECE // cuts
+            for s in range(cuts):
+                for b in range(H2 // P):
+                    o_ps = psum.tile([P, PIECE], F32, name="product")
+                    for k in range(H1 // P):
+                        nc.tensor.matmul(
+                            o_ps[:, :width],
+                            w2_blocks[:, k, b, :],
+                            h_bf[c][:, k, s * width : (s + 1) * width],
+                            start=(k == 0),
+                            stop=(k == H1 // P - 1),
+                        )
+                    o_sb = work.tile([P, PIECE], F32, name="o_sb")
+                    bias_lrelu(nc, work, o_sb[:, :width], o_ps[:, :width], b2_sb[:, b : b + 1])
+                    first = c * PIECE + s * width
+                    nc.sync.dma_start(out_blocks[:, b, first : first + width], o_sb[:, :width])

@@ -25,6 +25,7 @@ def tile_textclassifier_kernel(tc, table, w, bv, w1, b1, w2, b2, offs, out):
     with (
         tc.tile_pool(name="held", bufs=1) as held,
         tc.tile_pool(name="work", bufs=4) as work,
+        tc.tile_pool(name="stored", bufs=6) as stored,
         tc.psum_pool(name="psum", bufs=8) as psum,
     ):
         offsets = held.tile([P, N // 16], U16, name="offsets")
@@ -104,7 +105,7 @@ def tile_textclassifier_kernel(tc, table, w, bv, w1, b1, w2, b2, offs, out):
                             start=(k == 0),
                             stop=(k == H1 // P - 1),
                         )
-                    o_sb = work.tile([P, PIECE], F32, name="o_sb")
+                    o_sb = stored.tile([P, PIECE], F32, name="o_sb")
                     bias_lrelu(nc, work, o_sb[:, :width], o_ps[:, :width], b2_sb[:, b : b + 1])
                     first = c * PIECE + s * width
                     nc.sync.dma_start(out_blocks[:, b, first : first + width], o_sb[:, :width])

@@ -28,10 +28,10 @@ def tile_textclassifier_kernel(tc, table, w, bv, w1, b1, w2, b2, offs, out):
         tc.tile_pool(name="stored", bufs=6) as stored,
         tc.psum_pool(name="psum", bufs=8) as psum,
     ):
-        offsets = held.tile([P, N // 16], U16, name="offsets")
-        nc.sync.dma_start(offsets[:], offs)
         table_sb = held.tile([P, S], BF16, name="table_sb")
         nc.sync.dma_start(table_sb[:], table)
+        offsets = held.tile([P, N // 16], U16, name="offsets")
+        nc.sync.dma_start(offsets[:], offs)
         w_sb = held.tile([P, M], BF16, name="w_sb")
         nc.scalar.dma_start(w_sb[:], w)
 
@@ -41,12 +41,12 @@ def tile_textclassifier_kernel(tc, table, w, bv, w1, b1, w2, b2, offs, out):
         w1_sb = held.tile([P, M // P, H1], BF16, name="w1_sb")
 
         b1_sb = held.tile([P, H1 // P], F32, name="b1_sb")
-        nc.sync.dma_start(b1_sb[:], b1.rearrange("(p b) o -> p (b o)", p=P))
+        nc.scalar.dma_start(b1_sb[:], b1.rearrange("(p b) o -> p (b o)", p=P))
         nc.sync.dma_start(w1_sb[:], w1.rearrange("(k p) n -> p k n", p=P))
         b2_sb = held.tile([P, H2 // P], F32, name="b2_sb")
         nc.scalar.dma_start(b2_sb[:], b2.rearrange("(p b) o -> p (b o)", p=P))
         w2_sb = held.tile([P, H1 // P, H2], BF16, name="w2_sb")
-        nc.scalar.dma_start(w2_sb[:], w2.rearrange("(p k) n -> p k n", p=P))
+        nc.sync.dma_start(w2_sb[:], w2.rearrange("(p k) n -> p k n", p=P))
         w1_blocks = w1_sb[:].rearrange("d k (p b) -> d k b p", p=P)
         w2_blocks = w2_sb[:].rearrange("d k (p b) -> d k b p", p=P)
         out_blocks = out.rearrange("(p b) n -> p b n", p=P)

@@ -95,17 +95,22 @@ def tile_textclassifier_kernel(tc, table, w, bv, w1, b1, w2, b2, offs, out):
             cuts = 2 if c == PIECES - 1 else 1
             width = PIECE // cuts
             for s in range(cuts):
-                for b in range(H2 // P):
-                    o_ps = psum.tile([P, PIECE], F32, name="product")
-                    for k in range(H1 // P):
-                        nc.tensor.matmul(
-                            o_ps[:, :width],
-                            w2_blocks[:, k, b, :],
-                            h_bf[c][:, k, s * width : (s + 1) * width],
-                            start=(k == 0),
-                            stop=(k == H1 // P - 1),
-                        )
+                blocks, steps = range(H2 // P), range(H1 // P)
+                if c == PIECES - 1 and s == 0:
+                    order = [(b, k) for k in steps for b in blocks]
+                else:
+                    order = [(b, k) for b in blocks for k in steps]
+                o_ps = [psum.tile([P, PIECE], F32, name="product") for b in blocks]
+                for b, k in order:
+                    nc.tensor.matmul(
+                        o_ps[b][:, :width],
+                        w2_blocks[:, k, b, :],
+                        h_bf[c][:, k, s * width : (s + 1) * width],
+                        start=(k == 0),
+                        stop=(k == H1 // P - 1),
+                    )
+                for b in blocks:
                     o_sb = stored.tile([P, PIECE], F32, name="o_sb")
-                    bias_lrelu(nc, work, o_sb[:, :width], o_ps[:, :width], b2_sb[:, b : b + 1])
+                    bias_lrelu(nc, work, o_sb[:, :width], o_ps[b][:, :width], b2_sb[:, b : b + 1])
                     first = c * PIECE + s * width
                     nc.sync.dma_start(out_blocks[:, b, first : first + width], o_sb[:, :width])

@@ -32,8 +32,9 @@ def tile_textclassifier_kernel(tc, table, w, bv, w1, b1, w2, b2, offs, out):
         nc.sync.dma_start(table_sb[:], table)
         offsets = held.tile([P, N // 16], U16, name="offsets")
         nc.sync.dma_start(offsets[:], offs)
-        w_sb = held.tile([P, M], BF16, name="w_sb")
-        nc.scalar.dma_start(w_sb[:], w)
+        w_sb = [held.tile([P, P], BF16, name=f"w_sb{m}") for m in range(M // P)]
+        nc.scalar.dma_start(w_sb[0][:], w[:, :P])
+        nc.sync.dma_start(w_sb[1][:], w[:, P:])
 
         bv_sb = held.tile([P, M // P], F32, name="bv_sb")
         with nc.allow_non_contiguous_dma(reason="bv has one element to a partition and block"):
@@ -68,7 +69,7 @@ def tile_textclassifier_kernel(tc, table, w, bv, w1, b1, w2, b2, offs, out):
                 v_ps = psum.tile([P, PIECE], F32, name="product")
                 nc.tensor.matmul(
                     v_ps[:],
-                    w_sb[:, m * P : (m + 1) * P],
+                    w_sb[m][:],
                     table_sb[:].indirect(offsets[:, c * (PIECE // 16) : (c + 1) * (PIECE // 16)]),
                     start=True,
                     stop=True,

@@ -64,6 +64,7 @@ def tile_textclassifier_kernel(tc, table, w, bv, w1, b1, w2, b2, offs, out):
         v_bf = [held.tile([P, M // P, PIECE], BF16, name=f"v_bf{c}") for c in range(PIECES)]
         h_bf = [held.tile([P, H1 // P, PIECE], BF16, name=f"h_bf{c}") for c in range(PIECES)]
 
+        halves = [slice(0, PIECE // 2), slice(PIECE // 2, PIECE)]
         for c in range(PIECES):
             for m in range(M // P):
                 v_ps = psum.tile([P, PIECE], F32, name="product")
@@ -77,19 +78,21 @@ def tile_textclassifier_kernel(tc, table, w, bv, w1, b1, w2, b2, offs, out):
                 if m % 2 == 0:
                     nc.scalar.activation(v_bf[c][:, m, :], v_ps[:], IDENTITY, bias=bv_sb[:, m : m + 1])
                 else:
-                    nc.vector.tensor_scalar(v_bf[c][:, m, :], v_ps[:], bv_sb[:, m : m + 1], None, ADD)
+                    for part in halves if c == 0 else [slice(0, PIECE)]:
+                        nc.vector.tensor_scalar(v_bf[c][:, m, part], v_ps[:, part], bv_sb[:, m : m + 1], None, ADD)
 
         for c in range(PIECES):
             for b in range(H1 // P):
                 h_ps = psum.tile([P, PIECE], F32, name="product")
-                for k in range(M // P):
-                    nc.tensor.matmul(
-                        h_ps[:],
-                        w1_blocks[:, k, b, :],
-                        v_bf[c][:, k, :],
-                        start=(k == 0),
-                        stop=(k == M // P - 1),
-                    )
+                for part in halves if c == 0 and b == 0 else [slice(0, PIECE)]:
+                    for k in range(M // P):
+                        nc.tensor.matmul(
+                            h_ps[:, part],
+                            w1_blocks[:, k, b, :],
+                            v_bf[c][:, k, part],
+                            start=(k == 0),
+                            stop=(k == M // P - 1),
+                        )
                 bias_lrelu(nc, work, h_bf[c][:, b, :], h_ps[:], b1_sb[:, b : b + 1])
 
         for c in range(PIECES):

import concourse.mybir as mybir

BF16, F32, U16 = mybir.dt.bfloat16, mybir.dt.float32, mybir.dt.uint16
IDENTITY = mybir.ActivationFunctionType.Identity
ADD, MULT, MAX = mybir.AluOpType.add, mybir.AluOpType.mult, mybir.AluOpType.max

P = 128
D, S, M, H1, H2, N = 128, 256, 256, 512, 256, 512
SLOPE = 0.01
PIECE = 256
PIECES = N // PIECE
WARM_UP = 14
FLOPS = 2 * N * (D * M + M * H1 + H1 * H2)


def bias_lrelu(nc, work, dest, product, bias_column):
    width = product.shape[1]
    shifted = work.tile([P, PIECE], F32, name="shifted")
    nc.scalar.activation(shifted[:, :width], product, IDENTITY, bias=bias_column)
    nc.vector.scalar_tensor_tensor(dest, shifted[:, :width], SLOPE, shifted[:, :width], MULT, MAX)


def tile_textclassifier_kernel(tc, table, w, bv, w1, b1, w2, b2, offs, out):
    nc = tc.nc
    with (
        tc.tile_pool(name="held", bufs=1) as held,
        tc.tile_pool(name="work", bufs=4) as work,
        tc.tile_pool(name="stored", bufs=6) as stored,
        tc.psum_pool(name="psum", bufs=8) as psum,
    ):
        table_sb = held.tile([P, S], BF16, name="table_sb")
        nc.sync.dma_start(table_sb[:], table)
        offsets = held.tile([P, N // 16], U16, name="offsets")
        nc.sync.dma_start(offsets[:], offs)
        w_sb = [held.tile([P, P], BF16, name=f"w_sb{m}") for m in range(M // P)]
        nc.scalar.dma_start(w_sb[0][:], w[:, :P])
        nc.sync.dma_start(w_sb[1][:], w[:, P:])

        bv_sb = held.tile([P, M // P], F32, name="bv_sb")
        with nc.allow_non_contiguous_dma(reason="bv has one element to a partition and block"):
            nc.scalar.dma_start(bv_sb[:], bv.rearrange("(k p) o -> p (k o)", p=P))
        w1_sb = held.tile([P, M // P, H1], BF16, name="w1_sb")

        b1_sb = held.tile([P, H1 // P], F32, name="b1_sb")
        nc.scalar.dma_start(b1_sb[:], b1.rearrange("(p b) o -> p (b o)", p=P))
        nc.sync.dma_start(w1_sb[:], w1.rearrange("(k p) n -> p k n", p=P))
        b2_sb = held.tile([P, H2 // P], F32, name="b2_sb")
        nc.scalar.dma_start(b2_sb[:], b2.rearrange("(p b) o -> p (b o)", p=P))
        w2_sb = held.tile([P, H1 // P, H2], BF16, name="w2_sb")
        nc.sync.dma_start(w2_sb[:], w2.rearrange("(p k) n -> p k n", p=P))
        w1_blocks = w1_sb[:].rearrange("d k (p b) -> d k b p", p=P)
        w2_blocks = w2_sb[:].rearrange("d k (p b) -> d k b p", p=P)
        out_blocks = out.rearrange("(p b) n -> p b n", p=P)

        zeros = held.tile([P, P], BF16, name="zeros")
        nc.vector.memset(zeros[:], 0.0)
        warm_ps = psum.tile([P, P], F32, name="product")
        for i in range(WARM_UP):
            nc.tensor.matmul(warm_ps[:], zeros[:], zeros[:], start=True, stop=True)

        first_act = held.tile([P, 1], F32, name="first_act")
        nc.scalar.activation(first_act[:], zeros[:, 0:1], IDENTITY)

        v_bf = [held.tile([P, M // P, PIECE], BF16, name=f"v_bf{c}") for c in range(PIECES)]
        h_bf = [held.tile([P, H1 // P, PIECE], BF16, name=f"h_bf{c}") for c in range(PIECES)]

        halves = [slice(0, PIECE // 2), slice(PIECE // 2, PIECE)]
        for c in range(PIECES):
            for m in range(M // P):
                v_ps = psum.tile([P, PIECE], F32, name="product")
                nc.tensor.matmul(
                    v_ps[:],
                    w_sb[m][:],
                    table_sb[:].indirect(offsets[:, c * (PIECE // 16) : (c + 1) * (PIECE // 16)]),
                    start=True,
                    stop=True,
                )
                if m % 2 == 0:
                    nc.scalar.activation(v_bf[c][:, m, :], v_ps[:], IDENTITY, bias=bv_sb[:, m : m + 1])
                else:
                    for part in halves if c == 0 else [slice(0, PIECE)]:
                        nc.vector.tensor_scalar(v_bf[c][:, m, part], v_ps[:, part], bv_sb[:, m : m + 1], None, ADD)

        for c in range(PIECES):
            for b in range(H1 // P):
                h_ps = psum.tile([P, PIECE], F32, name="product")
                for part in halves if c == 0 and b == 0 else [slice(0, PIECE)]:
                    for k in range(M // P):
                        nc.tensor.matmul(
                            h_ps[:, part],
                            w1_blocks[:, k, b, :],
                            v_bf[c][:, k, part],
                            start=(k == 0),
                            stop=(k == M // P - 1),
                        )
                bias_lrelu(nc, work, h_bf[c][:, b, :], h_ps[:], b1_sb[:, b : b + 1])

        for c in range(PIECES):
            cuts = 2 if c == PIECES - 1 else 1
            width = PIECE // cuts
            for s in range(cuts):
                blocks, steps = range(H2 // P), range(H1 // P)
                if c == PIECES - 1 and s == 0:
                    order = [(b, k) for k in steps for b in blocks]
                else:
                    order = [(b, k) for b in blocks for k in steps]
                o_ps = [psum.tile([P, PIECE], F32, name="product") for b in blocks]
                for b, k in order:
                    nc.tensor.matmul(
                        o_ps[b][:, :width],
                        w2_blocks[:, k, b, :],
                        h_bf[c][:, k, s * width : (s + 1) * width],
                        start=(k == 0),
                        stop=(k == H1 // P - 1),
                    )
                for b in blocks:
                    o_sb = stored.tile([P, PIECE], F32, name="o_sb")
                    bias_lrelu(nc, work, o_sb[:, :width], o_ps[b][:, :width], b2_sb[:, b : b + 1])
                    first = c * PIECE + s * width
                    nc.sync.dma_start(out_blocks[:, b, first : first + width], o_sb[:, :width])
